import numpy as np
import ml_dtypes


def mxq(x, axis, fmt="e4m3"):
    dtype, down = {"e4m3": (ml_dtypes.float8_e4m3fn, 7), "e5m2": (ml_dtypes.float8_e5m2, 14)}[fmt]
    v = np.moveaxis(np.asarray(x, np.float32).astype(ml_dtypes.bfloat16).astype(np.float64), axis, -1)
    blocks = v.reshape(v.shape[:-1] + (-1, 32))
    amax = np.abs(blocks).max(-1, keepdims=True)
    byte = np.maximum(np.where(amax > 0, np.frexp(amax)[1] - 1 + 127, 0) - down, 1)
    scale = np.exp2(byte - 127.0)
    codes = (blocks / scale).astype(np.float32).astype(dtype).astype(np.float64)
    return np.moveaxis((codes * scale).reshape(v.shape), -1, axis)


WIDE = False


def mx_kscale(k):
    if not WIDE:
        return np.ones(k)
    levels = np.array([10, -10, 5, -5, 0])
    if k % 512:
        return np.exp2(np.random.permutation(np.resize(levels, k // 32))).repeat(32)
    a = np.empty((k // 512, 16))
    for p in range(k // 512):
        a[p, :8] = np.random.permutation(np.resize(levels, 8))
        for g in range(8):
            far = levels[np.abs(levels - a[p, g]) >= 10]
            a[p, g + 8] = far[np.random.randint(len(far))]
    return np.exp2(a.ravel()).repeat(32)


BF16 = ml_dtypes.bfloat16


def bf(x):
    return np.asarray(x, np.float32).astype(BF16)


def f64(x):
    return np.asarray(x).astype(np.float64)


B, N, E, L, A, H1, H2, G = 512, 8, 8, 512, 128, 1024, 512, 8


def mish(v):
    return v * np.tanh(np.log(1.0 + np.exp(v)))


def simnorm(v):
    vg = v.reshape(v.shape[:-1] + (v.shape[-1] // G, G))
    ex = np.exp(vg - vg.max(-1, keepdims=True))
    return (ex / ex.sum(-1, keepdims=True)).reshape(v.shape)


def softmax_last(v):
    ex = np.exp(v - v.max(-1, keepdims=True))
    return ex / ex.sum(-1, keepdims=True)


def setup_inputs():
    s = mx_kscale(B)[:, None, None]
    u = np.repeat(mx_kscale(L)[::G], G)
    r = np.random.standard_normal
    h20 = bf(mish(r((B, E, H2))))
    logits = bf(r((B, N, E)))
    W30 = bf(r((E, H2, L)) * 2.0 / np.sqrt(H2))
    b3 = bf(0.3 * r((E, L)))
    g = bf(r((B, N, L)) * np.exp2(np.random.randint(-6, 1, (B, N, 1))) * 16.0 / s * u)
    z = f64(h20).transpose(1, 0, 2) @ f64(W30) + f64(b3)[:, None, :]
    y = np.ascontiguousarray(simnorm(z).transpose(1, 0, 2))
    return {"h2": bf(f64(h20) * s), "logits": logits, "W3": bf(f64(W30) / u), "b3": b3,
            "y": np.asarray(y, np.float32), "grad_out": g}


def reference(h2, logits, W3, b3, y, grad_out):
    comb = softmax_last(f64(logits))
    g = f64(grad_out)
    dy = sum(comb[:, n, :, None] * g[:, n, None, :] for n in range(N))
    yf = f64(y)
    p = (yf * dy).reshape(B, E, L // G, G).sum(-1, keepdims=True)
    dz = (yf.reshape(B, E, L // G, G) * (dy.reshape(B, E, L // G, G) - p)).reshape(B, E, L)
    dzt = dz.transpose(1, 0, 2)
    ht = f64(h2).transpose(1, 0, 2)
    dx = mxq(dzt, 2, "e5m2") @ mxq(f64(W3), 2, "e4m3").transpose(0, 2, 1)
    dw = mxq(ht, 1, "e4m3").transpose(0, 2, 1) @ mxq(dzt, 1, "e5m2")
    return dx.transpose(1, 0, 2), dw

@@ -1,0 +1,244 @@
+from contextlib import ExitStack
+
+import concourse.mybir as mybir
+from concourse.masks import make_identity
+
+B, NA, E, L, H, GRP = 512, 8, 8, 512, 512, 8
+FLOPS = 2 * 2 * E * B * L * H + 2 * B * NA * E * L
+
+F32 = mybir.dt.float32
+BF16 = mybir.dt.bfloat16
+U32 = mybir.dt.uint32
+U8 = mybir.dt.uint8
+E4 = mybir.dt.float8_e4m3fn_x4
+E5 = mybir.dt.float8_e5m2_x4
+ALU = mybir.AluOpType
+AX = mybir.AxisListType
+ACT = mybir.ActivationFunctionType
+
+P = 128
+TOK = 16
+NPAIR = 12
+BV = 2 * TOK * NPAIR
+NG = L // GRP
+
+
+def tile_softmoedynamics_pb_v_kernel(tc, h2, logits, W3, b3, y, grad_out, out_0, out_1):
+    nc = tc.nc
+    with ExitStack() as ctx:
+        keep = ctx.enter_context(tc.tile_pool(name="keep", bufs=1))
+        st = ctx.enter_context(tc.tile_pool(name="st", bufs=2))
+        ps = ctx.enter_context(tc.psum_pool(name="ps", bufs=2))
+
+        warm = keep.tile([P, 1], F32, name="warm")
+        nc.vector.memset(warm[:], 0.0)
+        nc.scalar.activation(out=warm[:], in_=warm[:], func=ACT.Exp)
+        ident_f = keep.tile([P, P], F32, name="ident_f")
+        make_identity(nc, ident_f[:])
+        ident_b = keep.tile([P, P], BF16, name="ident_b")
+        make_identity(nc, ident_b[:])
+
+        lg = keep.tile([P, 2 * NPAIR + NA, E], BF16, name="lg")
+        nc.sync.dma_start(out=lg[:, 0 : 2 * NPAIR, :], in_=logits[0:BV].rearrange("(i b) n e -> (b n) i e", b=TOK))
+        nc.sync.dma_start(out=lg[:, 2 * NPAIR :, :], in_=logits[BV:B])
+
+        g_t = {}
+        y_t = {}
+
+        def load_pair(j):
+            g = st.tile([P, 2, L], BF16, name="g", tag="g", bufs=4)
+            nc.sync.dma_start(out=g[:], in_=grad_out[32 * j : 32 * j + 32].rearrange("(a b) n l -> (b n) a l", b=TOK))
+            yy = st.tile([P, 2, L], F32, name="yy", tag="y", bufs=4)
+            nc.sync.dma_start(out=yy[:], in_=y[32 * j : 32 * j + 32].rearrange("(a b) e l -> (b e) a l", b=TOK))
+            g_t[j] = g
+            y_t[j] = yy
+
+        w_raw = {}
+
+        def load_w(e):
+            w = st.tile([P, 4, L], BF16, name="w_raw", tag="w_raw", bufs=2)
+            nc.sync.dma_start(out=w[:], in_=W3[e].rearrange("(q p) l -> p q l", p=P))
+            w_raw[e] = w
+
+        h_raw = {}
+
+        def load_h(e):
+            hh = st.tile([P, 4, H], BF16, name="h_raw", tag="h_raw", bufs=2)
+            nc.sync.dma_start(out=hh[:], in_=h2[:, e, :].rearrange("(p j) h -> p j h", j=4))
+            h_raw[e] = hh
+
+        load_pair(0)
+        g_v = keep.tile([P, NA, L], BF16, name="g_v")
+        nc.sync.dma_start(out=g_v[:], in_=grad_out[BV:B])
+        load_pair(1)
+        y_v = keep.tile([P, E, L], F32, name="y_v")
+        load_w(0)
+        load_pair(2)
+        load_w(1)
+
+        NC_ = 2 * NPAIR + NA
+        mx = keep.tile([P, NC_], F32, name="mx")
+        nc.vector.tensor_reduce(out=mx[:], in_=lg[:], axis=AX.X, op=ALU.max)
+        sh = keep.tile([P, NC_, E], F32, name="sh")
+        nc.vector.tensor_tensor(out=sh[:], in0=lg[:], in1=mx[:].unsqueeze(2).to_broadcast([P, NC_, E]), op=ALU.subtract)
+        ex = keep.tile([P, NC_, E], F32, name="ex")
+        nc.scalar.activation(out=ex[:], in_=sh[:], func=ACT.Exp)
+        sm = keep.tile([P, NC_], F32, name="sm")
+        nc.vector.tensor_reduce(out=sm[:], in_=ex[:], axis=AX.X, op=ALU.add)
+        rc = keep.tile([P, NC_], F32, name="rc")
+        nc.vector.reciprocal(out=rc[:], in_=sm[:])
+        cb = keep.tile([P, NC_, E], F32, name="cb")
+        nc.vector.tensor_tensor(out=cb[:], in0=ex[:], in1=rc[:].unsqueeze(2).to_broadcast([P, NC_, E]), op=ALU.mult)
+
+        mask16 = keep.tile([P, TOK], F32, name="mask16")
+        nc.vector.tensor_reduce(out=mask16[:], in_=ident_f[:].rearrange("p (b n) -> p b n", n=NA), axis=AX.X, op=ALU.add)
+        bd = keep.tile([P, 2 * NPAIR, P], F32, name="bd")
+        CH = 4
+        for c0 in range(0, 2 * NPAIR, CH):
+            eng = nc.vector if c0 < 2 * CH else nc.gpsimd
+            eng.tensor_tensor(
+                out=bd[:, c0 : c0 + CH, :].rearrange("p i (b e) -> p i b e", e=E),
+                in0=mask16[:].unsqueeze(1).unsqueeze(3).to_broadcast([P, CH, TOK, E]),
+                in1=cb[:, c0 : c0 + CH, :].unsqueeze(2).to_broadcast([P, CH, TOK, E]),
+                op=ALU.mult,
+            )
+
+        a_grp = keep.tile([P, E, B, 4], BF16, name="a_grp", align_bytes=64)
+        a_words = a_grp[:].bitcast(F32)
+        w_codes = keep.tile([P, E, H], U32, name="w_codes", align_bytes=64)
+        w_scales = keep.tile([P, E, H], U8, name="w_scales", align_bytes=64)
+        h_codes = keep.tile([P, E, H], U32, name="h_codes", align_bytes=64)
+        h_scales = keep.tile([P, E, H], U8, name="h_scales", align_bytes=64)
+
+        def finish_dz(t, yy):
+            tf = t[:].rearrange("p a l -> p (a l)")
+            pr = ps.tile([P, 2, P], F32, name="pr", tag="pr", bufs=2)
+            for r in range(GRP):
+                nc.tensor.matmul(pr[:, 0, :], lhsT=tf[:, r : 2 * L : GRP], rhs=ident_f[:], is_transpose=True, start=(r == 0), stop=(r == GRP - 1))
+            pT = st.tile([P, P], F32, name="pT", tag="pT", bufs=2)
+            nc.scalar.copy(out=pT[:], in_=pr[:, 0, :])
+            nc.tensor.transpose(pr[:, 1, :], pT[:], ident_f[:])
+            s = st.tile([P, 2, L], F32, name="s", tag="s", bufs=2)
+            nc.vector.tensor_tensor(
+                out=s[:].rearrange("p a (g r) -> p (a g) r", r=GRP),
+                in0=yy.rearrange("p a (g r) -> p (a g) r", r=GRP),
+                in1=pr[:, 1, :].unsqueeze(2).to_broadcast([P, 2 * NG, GRP]),
+                op=ALU.mult,
+            )
+            dz = st.tile([P, 2, L], BF16, name="dz", tag="dz", bufs=3)
+            nc.gpsimd.tensor_tensor(out=dz[:], in0=t[:], in1=s[:], op=ALU.subtract)
+            return dz
+
+        def to_features(dz):
+            words = dz[:].rearrange("p a l -> p (a l)").bitcast(F32)
+            tr = ps.tile([P, 2, 2 * P], F32, name="tr", tag="tr", bufs=2)
+            for a in range(2):
+                for u in range(2):
+                    nc.tensor.transpose(tr[:, u, P * a : P * (a + 1)], words[:, 256 * a + u : 256 * (a + 1) : 2], ident_f[:])
+            return tr
+
+        def pe_pair(j):
+            g, yy = g_t.pop(j), y_t.pop(j)
+            t = st.tile([P, 2, L], F32, name="t", tag="t", bufs=3)
+            for a in range(2):
+                g32 = st.tile([P, L], F32, name="g32", tag="g32", bufs=3)
+                nc.scalar.copy(out=g32[:], in_=g[:, a, :])
+                dy = ps.tile([P, L], F32, name="dy", tag="acc", bufs=2)
+                nc.tensor.matmul(dy[:], lhsT=bd[:, 2 * j + a, :], rhs=g32[:], start=True, stop=True)
+                nc.vector.tensor_tensor(out=t[:, a, :], in0=dy[:], in1=yy[:, a, :], op=ALU.mult)
+            dz = finish_dz(t, yy[:])
+            tr = to_features(dz)
+            nc.scalar.copy(out=a_words[:, :, 32 * j : 32 * j + 32, :], in_=tr[:].rearrange("p u (c e) -> p e c u", e=E))
+
+        def w_prep(e):
+            words = w_raw.pop(e)[:].rearrange("p q l -> p (q l)").bitcast(F32)
+            w_grp = st.tile([P, H, 4], BF16, name="w_grp", tag="grp", bufs=3, align_bytes=64)
+            for k in range(2):
+                tr = ps.tile([P, 2, 2 * P], F32, name="tr", tag="tr", bufs=2)
+                for a in range(2):
+                    q = 2 * k + a
+                    for u in range(2):
+                        nc.tensor.transpose(tr[:, u, P * a : P * (a + 1)], words[:, 256 * q + u : 256 * (q + 1) : 2], ident_f[:])
+                nc.scalar.copy(out=w_grp[:].bitcast(F32)[:, 256 * k : 256 * (k + 1), :], in_=tr[:].rearrange("p u c -> p c u"))
+            nc.vector.quantize_mx(out=w_codes[:, e, :].bitcast(E4), scales=w_scales[:, e, :], in_=w_grp[:].rearrange("p h t -> p (h t)"))
+
+        def h_prep(e):
+            h_grp = st.tile([P, H, 4], BF16, name="h_grp", tag="grp", bufs=3, align_bytes=64)
+            nc.gpsimd.tensor_scalar(out=h_grp[:], in0=h_raw.pop(e)[:].rearrange("p j h -> p h j"), scalar1=1.0, scalar2=0.0, op0=ALU.mult, op1=ALU.add)
+            nc.vector.quantize_mx(out=h_codes[:, e, :].bitcast(E4), scales=h_scales[:, e, :], in_=h_grp[:].rearrange("p h t -> p (h t)"))
+
+        def leave(acc, dram, k):
+            o = st.tile([P, 512], F32, name="o", tag="o", bufs=4)
+            if k == 0:
+                nc.scalar.copy(out=o[:], in_=acc[:])
+                nc.scalar.dma_start(out=dram, in_=o[:])
+            else:
+                nc.vector.tensor_copy(out=o[:], in_=acc[:])
+                nc.sync.dma_start(out=dram, in_=o[:])
+
+        def out0(beta, e, k):
+            blk = slice(P * beta, P * (beta + 1))
+            a_codes = st.tile([P, P], U32, name="a_codes", tag="a_codes", bufs=4, align_bytes=64)
+            a_scales = st.tile([P, P], U8, name="a_scales", tag="a_scales", bufs=4, align_bytes=64)
+            nc.vector.quantize_mx(out=a_codes[:].bitcast(E5), scales=a_scales[:], in_=a_grp[:, e, blk, :].rearrange("p b t -> p (b t)"))
+            acc = ps.tile([P, H], F32, name="acc0", tag="mx", bufs=2)
+            nc.tensor.matmul_mx(out=acc[:], lhsT=a_codes[:].bitcast(E5), lhsT_scale=a_scales[:], rhs=w_codes[:, e, :].bitcast(E4), rhs_scale=w_scales[:, e, :], start=True, stop=True)
+            leave(acc, out_0[blk, e, :], k)
+
+        def out1(e):
+            b_grp = st.tile([P, L, 4], BF16, name="b_grp", tag="grp", bufs=3, align_bytes=64)
+            b_view = b_grp[:].rearrange("p (q t) s -> p q t s", t=4)
+            for k in range(2):
+                tb = ps.tile([P, 8, P], BF16, name="tb", tag="acc", bufs=2)
+                for t2 in range(2):
+                    for s in range(4):
+                        nc.tensor.transpose(tb[:, 4 * t2 + s, :], a_grp[:, e, s:B:4, 2 * k + t2], ident_b[:])
+                nc.scalar.copy(out=b_view[:, :, 2 * k : 2 * k + 2, :], in_=tb[:].rearrange("p (t s) q -> p q t s", s=4))
+            b_codes = st.tile([P, L], U32, name="b_codes", tag="b_codes", bufs=2, align_bytes=64)
+            b_scales = st.tile([P, L], U8, name="b_scales", tag="b_scales", bufs=2, align_bytes=64)
+            nc.vector.quantize_mx(out=b_codes[:].bitcast(E5), scales=b_scales[:], in_=b_grp[:].rearrange("p l s -> p (l s)"))
+            for q in range(4):
+                hs = slice(P * q, P * (q + 1))
+                acc = ps.tile([P, L], F32, name="acc1", tag="mx", bufs=2)
+                nc.tensor.matmul_mx(out=acc[:], lhsT=h_codes[:, e, hs].bitcast(E4), lhsT_scale=h_scales[:, e, hs], rhs=b_codes[:].bitcast(E5), rhs_scale=b_scales[:], start=True, stop=True)
+                leave(acc, out_1[e, hs, :], 1 if q == 3 else 0)
+
+        for j in range(NPAIR):
+            if j + 3 < NPAIR:
+                load_pair(j + 3)
+            if j == 1:
+                nc.sync.dma_start(out=y_v[:], in_=y[BV:B])
+            pe_pair(j)
+            if j < 4:
+                for e in (2 * j, 2 * j + 1):
+                    w_prep(e)
+                    if e + 2 < E:
+                        load_w(e + 2)
+                    else:
+                        load_h(e + 2 - E)
+            else:
+                h_prep(j - 4)
+                if j - 4 + 2 < E:
+                    load_h(j - 4 + 2)
+            if j % 4 == 3:
+                for e in range(E):
+                    out0(j // 4, e, 0)
+
+        for ep in range(E // 2):
+            yv = y_v[:, 2 * ep : 2 * ep + 2, :]
+            dyv = st.tile([P, 2, L], F32, name="dyv", tag="dyv", bufs=3)
+            for n in range(NA):
+                for a in range(2):
+                    c = cb[:, 2 * NPAIR + n, 2 * ep + a : 2 * ep + a + 1]
+                    if n == 0:
+                        nc.vector.tensor_scalar(out=dyv[:, a, :], in0=g_v[:, n, :], scalar1=c, scalar2=None, op0=ALU.mult)
+                    else:
+                        nc.vector.scalar_tensor_tensor(out=dyv[:, a, :], in0=g_v[:, n, :], scalar=c, in1=dyv[:, a, :], op0=ALU.mult, op1=ALU.add)
+            t = st.tile([P, 2, L], F32, name="t", tag="t", bufs=3)
+            nc.gpsimd.tensor_tensor(out=t[:], in0=dyv[:], in1=yv, op=ALU.mult)
+            dz = finish_dz(t, yv)
+            tr = to_features(dz)
+            nc.scalar.copy(out=a_words[:, 2 * ep : 2 * ep + 2, BV:B, :], in_=tr[:].rearrange("p u (a b) -> p a b u", a=2))
+            for a in range(2):
+                out0(3, 2 * ep + a, 0)
+                out1(2 * ep + a)

@@ -111,22 +111,28 @@ def tile_softmoedynamics_pb_v_kernel(tc, h2, logits, W3, b3, y, grad_out, out_0,
         h_scales = keep.tile([P, E, H], U8, name="h_scales", align_bytes=64)
 
         def finish_dz(t, yy):
-            tf = t[:].rearrange("p a l -> p (a l)")
+            tf = t[:].rearrange("p h a x -> p (h a x)")
             pr = ps.tile([P, 2, P], F32, name="pr", tag="pr", bufs=2)
             for r in range(GRP):
-                nc.tensor.matmul(pr[:, 0, :], lhsT=tf[:, r : 2 * L : GRP], rhs=ident_f[:], is_transpose=True, start=(r == 0), stop=(r == GRP - 1))
+                h, w = r // 2, r % 2
+                nc.tensor.matmul(pr[:, 0, :], lhsT=tf[:, 256 * h + w : 256 * (h + 1) : 2], rhs=ident_f[:], is_transpose=True, start=(r == 0), stop=(r == GRP - 1))
             pT = st.tile([P, P], F32, name="pT", tag="pT", bufs=2)
             nc.scalar.copy(out=pT[:], in_=pr[:, 0, :])
             nc.tensor.transpose(pr[:, 1, :], pT[:], ident_f[:])
-            s = st.tile([P, 2, L], F32, name="s", tag="s", bufs=2)
+            s = st.tile([P, 4, P, 2], F32, name="s", tag="s", bufs=2)
             nc.vector.tensor_tensor(
-                out=s[:].rearrange("p a (g r) -> p (a g) r", r=GRP),
-                in0=yy.rearrange("p a (g r) -> p (a g) r", r=GRP),
-                in1=pr[:, 1, :].unsqueeze(2).to_broadcast([P, 2 * NG, GRP]),
+                out=s[:],
+                in0=yy.rearrange("p a (g h w) -> p h (a g) w", h=4, w=2),
+                in1=pr[:, 1, :].unsqueeze(1).unsqueeze(3).to_broadcast([P, 4, P, 2]),
                 op=ALU.mult,
             )
             dz = st.tile([P, 2, L], BF16, name="dz", tag="dz", bufs=3)
-            nc.gpsimd.tensor_tensor(out=dz[:], in0=t[:], in1=s[:], op=ALU.subtract)
+            nc.vector.tensor_tensor(
+                out=dz[:].rearrange("p a (g h w) -> p (a g) h w", h=4, w=2),
+                in0=t[:].rearrange("p h a (g w) -> p (a g) h w", w=2),
+                in1=s[:].rearrange("p h x w -> p x h w"),
+                op=ALU.subtract,
+            )
             return dz
 
         def to_features(dz):
@@ -139,13 +145,18 @@ def tile_softmoedynamics_pb_v_kernel(tc, h2, logits, W3, b3, y, grad_out, out_0,
 
         def pe_pair(j):
             g, yy = g_t.pop(j), y_t.pop(j)
-            t = st.tile([P, 2, L], F32, name="t", tag="t", bufs=3)
+            t = st.tile([P, 4, 2, P], F32, name="t", tag="t", bufs=3)
             for a in range(2):
                 g32 = st.tile([P, L], F32, name="g32", tag="g32", bufs=3)
-                nc.scalar.copy(out=g32[:], in_=g[:, a, :])
+                nc.scalar.copy(out=g32[:].rearrange("p (h g w) -> p h g w", h=4, w=2), in_=g[:, a, :].rearrange("p (g h w) -> p h g w", h=4, w=2))
                 dy = ps.tile([P, L], F32, name="dy", tag="acc", bufs=2)
                 nc.tensor.matmul(dy[:], lhsT=bd[:, 2 * j + a, :], rhs=g32[:], start=True, stop=True)
-                nc.vector.tensor_tensor(out=t[:, a, :], in0=dy[:], in1=yy[:, a, :], op=ALU.mult)
+                nc.vector.tensor_tensor(
+                    out=t[:, :, a, :].rearrange("p h (g w) -> p h g w", w=2),
+                    in0=dy[:].rearrange("p (h g w) -> p h g w", h=4, w=2),
+                    in1=yy[:, a, :].rearrange("p (g h w) -> p h g w", h=4, w=2),
+                    op=ALU.mult,
+                )
             dz = finish_dz(t, yy[:])
             tr = to_features(dz)
             nc.scalar.copy(out=a_words[:, :, 32 * j : 32 * j + 32, :], in_=tr[:].rearrange("p u (c e) -> p e c u", e=E))
@@ -164,7 +175,10 @@ def tile_softmoedynamics_pb_v_kernel(tc, h2, logits, W3, b3, y, grad_out, out_0,
 
         def h_prep(e):
             h_grp = st.tile([P, H, 4], BF16, name="h_grp", tag="grp", bufs=3, align_bytes=64)
-            nc.gpsimd.tensor_scalar(out=h_grp[:], in0=h_raw.pop(e)[:].rearrange("p j h -> p h j"), scalar1=1.0, scalar2=0.0, op0=ALU.mult, op1=ALU.add)
+            if e < 6:
+                nc.scalar.copy(out=h_grp[:], in_=h_raw.pop(e)[:].rearrange("p j h -> p h j"))
+            else:
+                nc.vector.tensor_copy(out=h_grp[:], in_=h_raw.pop(e)[:].rearrange("p j h -> p h j"))
             nc.vector.quantize_mx(out=h_codes[:, e, :].bitcast(E4), scales=h_scales[:, e, :], in_=h_grp[:].rearrange("p h t -> p (h t)"))
 
         def leave(acc, dram, k):
@@ -234,8 +248,13 @@ def tile_softmoedynamics_pb_v_kernel(tc, h2, logits, W3, b3, y, grad_out, out_0,
                         nc.vector.tensor_scalar(out=dyv[:, a, :], in0=g_v[:, n, :], scalar1=c, scalar2=None, op0=ALU.mult)
                     else:
                         nc.vector.scalar_tensor_tensor(out=dyv[:, a, :], in0=g_v[:, n, :], scalar=c, in1=dyv[:, a, :], op0=ALU.mult, op1=ALU.add)
-            t = st.tile([P, 2, L], F32, name="t", tag="t", bufs=3)
-            nc.gpsimd.tensor_tensor(out=t[:], in0=dyv[:], in1=yv, op=ALU.mult)
+            t = st.tile([P, 4, 2, P], F32, name="t", tag="t", bufs=3)
+            nc.vector.tensor_tensor(
+                out=t[:].rearrange("p h a (g w) -> p h (a g) w", w=2),
+                in0=dyv[:].rearrange("p a (g h w) -> p h (a g) w", h=4, w=2),
+                in1=yv.rearrange("p a (g h w) -> p h (a g) w", h=4, w=2),
+                op=ALU.mult,
+            )
             dz = finish_dz(t, yv)
             tr = to_features(dz)
             nc.scalar.copy(out=a_words[:, 2 * ep : 2 * ep + 2, BV:B, :], in_=tr[:].rearrange("p u (a b) -> p a b u", a=2))

@@ -35,15 +35,16 @@ def tile_softmoedynamics_pb_v_kernel(tc, h2, logits, W3, b3, y, grad_out, out_0,
         nc.scalar.activation(out=warm[:], in_=warm[:], func=ACT.Exp)
         ident_f = keep.tile([P, P], F32, name="ident_f")
         make_identity(nc, ident_f[:])
-        ident_b = keep.tile([P, P], BF16, name="ident_b")
-        make_identity(nc, ident_b[:])
+        swap_f = keep.tile([P, P], F32, name="swap_f")
+        for w in range(2):
+            nc.vector.tensor_copy(out=swap_f[:, w:P:2], in_=ident_f[:, 1 - w : P : 2])
 
-        lg = keep.tile([P, 2 * NPAIR + NA, E], BF16, name="lg")
+        NCOL = 2 * NPAIR + NA
+        lg = keep.tile([P, NCOL, E], BF16, name="lg")
         nc.sync.dma_start(out=lg[:, 0 : 2 * NPAIR, :], in_=logits[0:BV].rearrange("(i b) n e -> (b n) i e", b=TOK))
         nc.sync.dma_start(out=lg[:, 2 * NPAIR :, :], in_=logits[BV:B])
 
-        g_t = {}
-        y_t = {}
+        g_t, y_t, w_raw, h_raw = {}, {}, {}, {}
 
         def load_pair(j):
             g = st.tile([P, 2, L], BF16, name="g", tag="g", bufs=4)
@@ -53,14 +54,10 @@ def tile_softmoedynamics_pb_v_kernel(tc, h2, logits, W3, b3, y, grad_out, out_0,
             g_t[j] = g
             y_t[j] = yy
 
-        w_raw = {}
-
         def load_w(e):
             w = st.tile([P, 4, L], BF16, name="w_raw", tag="w_raw", bufs=2)
             nc.sync.dma_start(out=w[:], in_=W3[e].rearrange("(q p) l -> p q l", p=P))
             w_raw[e] = w
-
-        h_raw = {}
 
         def load_h(e):
             hh = st.tile([P, 4, H], BF16, name="h_raw", tag="h_raw", bufs=2)
@@ -71,24 +68,22 @@ def tile_softmoedynamics_pb_v_kernel(tc, h2, logits, W3, b3, y, grad_out, out_0,
         g_v = keep.tile([P, NA, L], BF16, name="g_v")
         nc.sync.dma_start(out=g_v[:], in_=grad_out[BV:B])
         load_pair(1)
-        y_v = keep.tile([P, E, L], F32, name="y_v")
         load_w(0)
         load_pair(2)
         load_w(1)
 
-        NC_ = 2 * NPAIR + NA
-        mx = keep.tile([P, NC_], F32, name="mx")
+        mx = keep.tile([P, NCOL], F32, name="mx")
         nc.vector.tensor_reduce(out=mx[:], in_=lg[:], axis=AX.X, op=ALU.max)
-        sh = keep.tile([P, NC_, E], F32, name="sh")
-        nc.vector.tensor_tensor(out=sh[:], in0=lg[:], in1=mx[:].unsqueeze(2).to_broadcast([P, NC_, E]), op=ALU.subtract)
-        ex = keep.tile([P, NC_, E], F32, name="ex")
+        sh = keep.tile([P, NCOL, E], F32, name="sh")
+        nc.vector.tensor_tensor(out=sh[:], in0=lg[:], in1=mx[:].unsqueeze(2).to_broadcast([P, NCOL, E]), op=ALU.subtract)
+        ex = keep.tile([P, NCOL, E], F32, name="ex")
         nc.scalar.activation(out=ex[:], in_=sh[:], func=ACT.Exp)
-        sm = keep.tile([P, NC_], F32, name="sm")
+        sm = keep.tile([P, NCOL], F32, name="sm")
         nc.vector.tensor_reduce(out=sm[:], in_=ex[:], axis=AX.X, op=ALU.add)
-        rc = keep.tile([P, NC_], F32, name="rc")
+        rc = keep.tile([P, NCOL], F32, name="rc")
         nc.vector.reciprocal(out=rc[:], in_=sm[:])
-        cb = keep.tile([P, NC_, E], F32, name="cb")
-        nc.vector.tensor_tensor(out=cb[:], in0=ex[:], in1=rc[:].unsqueeze(2).to_broadcast([P, NC_, E]), op=ALU.mult)
+        cb = keep.tile([P, NCOL, E], F32, name="cb")
+        nc.vector.tensor_tensor(out=cb[:], in0=ex[:], in1=rc[:].unsqueeze(2).to_broadcast([P, NCOL, E]), op=ALU.mult)
 
         mask16 = keep.tile([P, TOK], F32, name="mask16")
         nc.vector.tensor_reduce(out=mask16[:], in_=ident_f[:].rearrange("p (b n) -> p b n", n=NA), axis=AX.X, op=ALU.add)
@@ -103,27 +98,27 @@ def tile_softmoedynamics_pb_v_kernel(tc, h2, logits, W3, b3, y, grad_out, out_0,
                 op=ALU.mult,
             )
 
-        a_grp = keep.tile([P, E, B, 4], BF16, name="a_grp", align_bytes=64)
-        a_words = a_grp[:].bitcast(F32)
+        a2 = keep.tile([P, E, 2, 4, P], F32, name="a2")
         w_codes = keep.tile([P, E, H], U32, name="w_codes", align_bytes=64)
         w_scales = keep.tile([P, E, H], U8, name="w_scales", align_bytes=64)
         h_codes = keep.tile([P, E, H], U32, name="h_codes", align_bytes=64)
         h_scales = keep.tile([P, E, H], U8, name="h_scales", align_bytes=64)
 
         def finish_dz(t, yy):
-            tf = t[:].rearrange("p h a x -> p (h a x)")
-            pr = ps.tile([P, 2, P], F32, name="pr", tag="pr", bufs=2)
-            for r in range(GRP):
-                h, w = r // 2, r % 2
-                nc.tensor.matmul(pr[:, 0, :], lhsT=tf[:, 256 * h + w : 256 * (h + 1) : 2], rhs=ident_f[:], is_transpose=True, start=(r == 0), stop=(r == GRP - 1))
-            pT = st.tile([P, P], F32, name="pT", tag="pT", bufs=2)
-            nc.scalar.copy(out=pT[:], in_=pr[:, 0, :])
-            nc.tensor.transpose(pr[:, 1, :], pT[:], ident_f[:])
+            pr = ps.tile([P, 4, P], F32, name="pr", tag="pr", bufs=2)
+            for a in range(2):
+                for h in range(4):
+                    nc.tensor.matmul(pr[:, a, :], lhsT=t[:, h, a, :], rhs=ident_f[:], is_transpose=True, start=(h == 0), stop=(h == 3))
+            pT = st.tile([P, 2, P], F32, name="pT", tag="pT", bufs=2)
+            nc.scalar.copy(out=pT[:], in_=pr[:, 0:2, :])
+            for a in range(2):
+                nc.tensor.matmul(pr[:, 2 + a, :], lhsT=pT[:, a, :], rhs=ident_f[:], is_transpose=True, start=True, stop=False)
+                nc.tensor.matmul(pr[:, 2 + a, :], lhsT=pT[:, a, :], rhs=swap_f[:], is_transpose=True, start=False, stop=True)
             s = st.tile([P, 4, P, 2], F32, name="s", tag="s", bufs=2)
             nc.vector.tensor_tensor(
                 out=s[:],
                 in0=yy.rearrange("p a (g h w) -> p h (a g) w", h=4, w=2),
-                in1=pr[:, 1, :].unsqueeze(1).unsqueeze(3).to_broadcast([P, 4, P, 2]),
+                in1=pr[:, 2:4, :].rearrange("p a (g w) -> p (a g) w", w=2).unsqueeze(1).to_broadcast([P, 4, P, 2]),
                 op=ALU.mult,
             )
             dz = st.tile([P, 2, L], BF16, name="dz", tag="dz", bufs=3)
@@ -143,6 +138,14 @@ def tile_softmoedynamics_pb_v_kernel(tc, h2, logits, W3, b3, y, grad_out, out_0,
                     nc.tensor.transpose(tr[:, u, P * a : P * (a + 1)], words[:, 256 * a + u : 256 * (a + 1) : 2], ident_f[:])
             return tr
 
+        ag_t = {}
+
+        def a_block(beta):
+            if beta not in ag_t:
+                a_new = st.tile([P, E, P, 4], BF16, name="a_grp", tag="a_grp", bufs=2, align_bytes=64)
+                ag_t[beta] = a_new
+            return ag_t[beta]
+
         def pe_pair(j):
             g, yy = g_t.pop(j), y_t.pop(j)
             t = st.tile([P, 4, 2, P], F32, name="t", tag="t", bufs=3)
@@ -159,7 +162,10 @@ def tile_softmoedynamics_pb_v_kernel(tc, h2, logits, W3, b3, y, grad_out, out_0,
                 )
             dz = finish_dz(t, yy[:])
             tr = to_features(dz)
-            nc.scalar.copy(out=a_words[:, :, 32 * j : 32 * j + 32, :], in_=tr[:].rearrange("p u (c e) -> p e c u", e=E))
+            c0 = 32 * (j % 4)
+            nc.scalar.copy(out=a_block(j // 4)[:].bitcast(F32)[:, :, c0 : c0 + 32, :], in_=tr[:].rearrange("p u (c e) -> p e c u", e=E))
+            for u in range(2):
+                nc.scalar.copy(out=a2[:, :, u, :, 8 * j : 8 * j + 8], in_=tr[:, u, :].rearrange("p (x s e) -> p e s x", s=4, e=E))
 
         def w_prep(e):
             words = w_raw.pop(e)[:].rearrange("p q l -> p (q l)").bitcast(F32)
@@ -181,33 +187,38 @@ def tile_softmoedynamics_pb_v_kernel(tc, h2, logits, W3, b3, y, grad_out, out_0,
                 nc.vector.tensor_copy(out=h_grp[:], in_=h_raw.pop(e)[:].rearrange("p j h -> p h j"))
             nc.vector.quantize_mx(out=h_codes[:, e, :].bitcast(E4), scales=h_scales[:, e, :], in_=h_grp[:].rearrange("p h t -> p (h t)"))
 
-        def leave(acc, dram, k):
-            o = st.tile([P, 512], F32, name="o", tag="o", bufs=4)
-            if k == 0:
-                nc.scalar.copy(out=o[:], in_=acc[:])
-                nc.scalar.dma_start(out=dram, in_=o[:])
-            else:
-                nc.vector.tensor_copy(out=o[:], in_=acc[:])
-                nc.sync.dma_start(out=dram, in_=o[:])
+        ac_t = {}
 
-        def out0(beta, e, k):
-            blk = slice(P * beta, P * (beta + 1))
-            a_codes = st.tile([P, P], U32, name="a_codes", tag="a_codes", bufs=4, align_bytes=64)
-            a_scales = st.tile([P, P], U8, name="a_scales", tag="a_scales", bufs=4, align_bytes=64)
-            nc.vector.quantize_mx(out=a_codes[:].bitcast(E5), scales=a_scales[:], in_=a_grp[:, e, blk, :].rearrange("p b t -> p (b t)"))
+        def a_quant(beta, e0, ne):
+            if beta not in ac_t:
+                c_new = st.tile([P, E, P], U32, name="a_codes", tag="a_codes", bufs=2, align_bytes=64)
+                s_new = st.tile([P, E, P], U8, name="a_scales", tag="a_scales", bufs=2, align_bytes=64)
+                ac_t[beta] = (c_new, s_new)
+            a_codes, a_scales = ac_t[beta]
+            nc.vector.quantize_mx(
+                out=a_codes[:, e0 : e0 + ne, :].rearrange("p e b -> p (e b)").bitcast(E5),
+                scales=a_scales[:, e0 : e0 + ne, :].rearrange("p e b -> p (e b)"),
+                in_=ag_t[beta][:, e0 : e0 + ne, :, :].rearrange("p e b t -> p (e b t)"),
+            )
+
+        def out0(beta, e):
+            a_codes, a_scales = ac_t[beta]
             acc = ps.tile([P, H], F32, name="acc0", tag="mx", bufs=2)
-            nc.tensor.matmul_mx(out=acc[:], lhsT=a_codes[:].bitcast(E5), lhsT_scale=a_scales[:], rhs=w_codes[:, e, :].bitcast(E4), rhs_scale=w_scales[:, e, :], start=True, stop=True)
-            leave(acc, out_0[blk, e, :], k)
+            nc.tensor.matmul_mx(out=acc[:], lhsT=a_codes[:, e, :].bitcast(E5), lhsT_scale=a_scales[:, e, :], rhs=w_codes[:, e, :].bitcast(E4), rhs_scale=w_scales[:, e, :], start=True, stop=True)
+            o = st.tile([P, H], F32, name="o", tag="o", bufs=4)
+            nc.scalar.copy(out=o[:], in_=acc[:])
+            nc.sync.dma_start(out=out_0[P * beta : P * (beta + 1), e, :], in_=o[:])
 
         def out1(e):
             b_grp = st.tile([P, L, 4], BF16, name="b_grp", tag="grp", bufs=3, align_bytes=64)
-            b_view = b_grp[:].rearrange("p (q t) s -> p q t s", t=4)
-            for k in range(2):
-                tb = ps.tile([P, 8, P], BF16, name="tb", tag="acc", bufs=2)
-                for t2 in range(2):
-                    for s in range(4):
-                        nc.tensor.transpose(tb[:, 4 * t2 + s, :], a_grp[:, e, s:B:4, 2 * k + t2], ident_b[:])
-                nc.scalar.copy(out=b_view[:, :, 2 * k : 2 * k + 2, :], in_=tb[:].rearrange("p (t s) q -> p q t s", s=4))
+            for u in range(2):
+                tb = ps.tile([P, 4, P], F32, name="tb", tag="acc", bufs=2)
+                for s in range(4):
+                    nc.tensor.transpose(tb[:, s, :], a2[:, e, u, s, :], ident_f[:])
+                nc.scalar.copy(
+                    out=b_grp[:, 256 * u : 256 * (u + 1), :].rearrange("p (q w) s -> p q w s", w=2),
+                    in_=tb[:].rearrange("p s q -> p (s q)").bitcast(BF16).rearrange("p (s q w) -> p q w s", s=4, w=2),
+                )
             b_codes = st.tile([P, L], U32, name="b_codes", tag="b_codes", bufs=2, align_bytes=64)
             b_scales = st.tile([P, L], U8, name="b_scales", tag="b_scales", bufs=2, align_bytes=64)
             nc.vector.quantize_mx(out=b_codes[:].bitcast(E5), scales=b_scales[:], in_=b_grp[:].rearrange("p l s -> p (l s)"))
@@ -215,13 +226,19 @@ def tile_softmoedynamics_pb_v_kernel(tc, h2, logits, W3, b3, y, grad_out, out_0,
                 hs = slice(P * q, P * (q + 1))
                 acc = ps.tile([P, L], F32, name="acc1", tag="mx", bufs=2)
                 nc.tensor.matmul_mx(out=acc[:], lhsT=h_codes[:, e, hs].bitcast(E4), lhsT_scale=h_scales[:, e, hs], rhs=b_codes[:].bitcast(E5), rhs_scale=b_scales[:], start=True, stop=True)
-                leave(acc, out_1[e, hs, :], 1 if q == 3 else 0)
+                o = st.tile([P, L], F32, name="o", tag="o", bufs=4)
+                src = acc[:].rearrange("p (u q w) -> p q u w", u=2, w=2)
+                dst = o[:].rearrange("p (q u w) -> p q u w", u=2, w=2)
+                if q == 3:
+                    nc.vector.tensor_copy(out=dst, in_=src)
+                    nc.sync.dma_start(out=out_1[e, hs, :], in_=o[:])
+                else:
+                    nc.scalar.copy(out=dst, in_=src)
+                    nc.sync.dma_start(out=out_1[e, hs, :], in_=o[:])
 
         for j in range(NPAIR):
             if j + 3 < NPAIR:
                 load_pair(j + 3)
-            if j == 1:
-                nc.sync.dma_start(out=y_v[:], in_=y[BV:B])
             pe_pair(j)
             if j < 4:
                 for e in (2 * j, 2 * j + 1):
@@ -235,11 +252,13 @@ def tile_softmoedynamics_pb_v_kernel(tc, h2, logits, W3, b3, y, grad_out, out_0,
                 if j - 4 + 2 < E:
                     load_h(j - 4 + 2)
             if j % 4 == 3:
+                a_quant(j // 4, 0, E)
                 for e in range(E):
-                    out0(j // 4, e, 0)
+                    out0(j // 4, e)
 
         for ep in range(E // 2):
-            yv = y_v[:, 2 * ep : 2 * ep + 2, :]
+            yv = st.tile([P, 2, L], F32, name="yv", tag="y", bufs=4)
+            nc.sync.dma_start(out=yv[:], in_=y[BV:B, 2 * ep : 2 * ep + 2, :])
             dyv = st.tile([P, 2, L], F32, name="dyv", tag="dyv", bufs=3)
             for n in range(NA):
                 for a in range(2):
@@ -252,12 +271,15 @@ def tile_softmoedynamics_pb_v_kernel(tc, h2, logits, W3, b3, y, grad_out, out_0,
             nc.vector.tensor_tensor(
                 out=t[:].rearrange("p h a (g w) -> p h (a g) w", w=2),
                 in0=dyv[:].rearrange("p a (g h w) -> p h (a g) w", h=4, w=2),
-                in1=yv.rearrange("p a (g h w) -> p h (a g) w", h=4, w=2),
+                in1=yv[:].rearrange("p a (g h w) -> p h (a g) w", h=4, w=2),
                 op=ALU.mult,
             )
-            dz = finish_dz(t, yv)
+            dz = finish_dz(t, yv[:])
             tr = to_features(dz)
-            nc.scalar.copy(out=a_words[:, 2 * ep : 2 * ep + 2, BV:B, :], in_=tr[:].rearrange("p u (a b) -> p a b u", a=2))
+            nc.scalar.copy(out=a_block(3)[:].bitcast(F32)[:, 2 * ep : 2 * ep + 2, :, :], in_=tr[:].rearrange("p u (a b) -> p a b u", a=2))
+            for u in range(2):
+                nc.scalar.copy(out=a2[:, 2 * ep : 2 * ep + 2, u, :, 96:P], in_=tr[:, u, :].rearrange("p (a x s) -> p a s x", a=2, s=4))
+            a_quant(3, 2 * ep, 2)
             for a in range(2):
-                out0(3, 2 * ep + a, 0)
+                out0(3, 2 * ep + a)
                 out1(2 * ep + a)

@@ -35,9 +35,6 @@ def tile_softmoedynamics_pb_v_kernel(tc, h2, logits, W3, b3, y, grad_out, out_0,
         nc.scalar.activation(out=warm[:], in_=warm[:], func=ACT.Exp)
         ident_f = keep.tile([P, P], F32, name="ident_f")
         make_identity(nc, ident_f[:])
-        swap_f = keep.tile([P, P], F32, name="swap_f")
-        for w in range(2):
-            nc.vector.tensor_copy(out=swap_f[:, w:P:2], in_=ident_f[:, 1 - w : P : 2])
 
         NCOL = 2 * NPAIR + NA
         lg = keep.tile([P, NCOL, E], BF16, name="lg")
@@ -64,13 +61,13 @@ def tile_softmoedynamics_pb_v_kernel(tc, h2, logits, W3, b3, y, grad_out, out_0,
             nc.sync.dma_start(out=hh[:], in_=h2[:, e, :].rearrange("(p j) h -> p j h", j=4))
             h_raw[e] = hh
 
+        load_w(0)
         load_pair(0)
+        load_w(1)
         g_v = keep.tile([P, NA, L], BF16, name="g_v")
         nc.sync.dma_start(out=g_v[:], in_=grad_out[BV:B])
         load_pair(1)
-        load_w(0)
         load_pair(2)
-        load_w(1)
 
         mx = keep.tile([P, NCOL], F32, name="mx")
         nc.vector.tensor_reduce(out=mx[:], in_=lg[:], axis=AX.X, op=ALU.max)
@@ -90,7 +87,7 @@ def tile_softmoedynamics_pb_v_kernel(tc, h2, logits, W3, b3, y, grad_out, out_0,
         bd = keep.tile([P, 2 * NPAIR, P], F32, name="bd")
         CH = 4
         for c0 in range(0, 2 * NPAIR, CH):
-            eng = nc.vector if c0 < 2 * CH else nc.gpsimd
+            eng = nc.vector if c0 < CH else nc.gpsimd
             eng.tensor_tensor(
                 out=bd[:, c0 : c0 + CH, :].rearrange("p i (b e) -> p i b e", e=E),
                 in0=mask16[:].unsqueeze(1).unsqueeze(3).to_broadcast([P, CH, TOK, E]),
@@ -112,13 +109,14 @@ def tile_softmoedynamics_pb_v_kernel(tc, h2, logits, W3, b3, y, grad_out, out_0,
             pT = st.tile([P, 2, P], F32, name="pT", tag="pT", bufs=2)
             nc.scalar.copy(out=pT[:], in_=pr[:, 0:2, :])
             for a in range(2):
-                nc.tensor.matmul(pr[:, 2 + a, :], lhsT=pT[:, a, :], rhs=ident_f[:], is_transpose=True, start=True, stop=False)
-                nc.tensor.matmul(pr[:, 2 + a, :], lhsT=pT[:, a, :], rhs=swap_f[:], is_transpose=True, start=False, stop=True)
+                nc.tensor.transpose(pr[:, 2 + a, :], pT[:, a, :], ident_f[:])
+            p = st.tile([P, P], F32, name="p", tag="p", bufs=2)
+            nc.vector.tensor_reduce(out=p[:], in_=pr[:, 2:4, :].rearrange("p a (g w) -> p (a g) w", w=2), axis=AX.X, op=ALU.add)
             s = st.tile([P, 4, P, 2], F32, name="s", tag="s", bufs=2)
             nc.vector.tensor_tensor(
                 out=s[:],
                 in0=yy.rearrange("p a (g h w) -> p h (a g) w", h=4, w=2),
-                in1=pr[:, 2:4, :].rearrange("p a (g w) -> p (a g) w", w=2).unsqueeze(1).to_broadcast([P, 4, P, 2]),
+                in1=p[:].unsqueeze(1).unsqueeze(3).to_broadcast([P, 4, P, 2]),
                 op=ALU.mult,
             )
             dz = st.tile([P, 2, L], BF16, name="dz", tag="dz", bufs=3)
@@ -181,10 +179,9 @@ def tile_softmoedynamics_pb_v_kernel(tc, h2, logits, W3, b3, y, grad_out, out_0,
 
         def h_prep(e):
             h_grp = st.tile([P, H, 4], BF16, name="h_grp", tag="grp", bufs=3, align_bytes=64)
-            if e < 6:
-                nc.scalar.copy(out=h_grp[:], in_=h_raw.pop(e)[:].rearrange("p j h -> p h j"))
-            else:
-                nc.vector.tensor_copy(out=h_grp[:], in_=h_raw.pop(e)[:].rearrange("p j h -> p h j"))
+            hr = h_raw.pop(e)
+            for c in range(4):
+                nc.gpsimd.tensor_scalar(out=h_grp[:, P * c : P * (c + 1), :], in0=hr[:, :, P * c : P * (c + 1)].rearrange("p j h -> p h j"), scalar1=1.0, scalar2=0.0, op0=ALU.mult, op1=ALU.add)
             nc.vector.quantize_mx(out=h_codes[:, e, :].bitcast(E4), scales=h_scales[:, e, :], in_=h_grp[:].rearrange("p h t -> p (h t)"))
 
         ac_t = {}
@@ -212,7 +209,7 @@ def tile_softmoedynamics_pb_v_kernel(tc, h2, logits, W3, b3, y, grad_out, out_0,
         def out1(e):
             b_grp = st.tile([P, L, 4], BF16, name="b_grp", tag="grp", bufs=3, align_bytes=64)
             for u in range(2):
-                tb = ps.tile([P, 4, P], F32, name="tb", tag="acc", bufs=2)
+                tb = ps.tile([P, 4, P], F32, name="tb", tag=("acc", "tr")[u], bufs=2)
                 for s in range(4):
                     nc.tensor.transpose(tb[:, s, :], a2[:, e, u, s, :], ident_f[:])
                 nc.scalar.copy(
@@ -224,17 +221,13 @@ def tile_softmoedynamics_pb_v_kernel(tc, h2, logits, W3, b3, y, grad_out, out_0,
             nc.vector.quantize_mx(out=b_codes[:].bitcast(E5), scales=b_scales[:], in_=b_grp[:].rearrange("p l s -> p (l s)"))
             for q in range(4):
                 hs = slice(P * q, P * (q + 1))
-                acc = ps.tile([P, L], F32, name="acc1", tag="mx", bufs=2)
+                acc = ps.tile([P, L], F32, name="acc1", tag=("mx", "pr")[q % 2], bufs=2)
                 nc.tensor.matmul_mx(out=acc[:], lhsT=h_codes[:, e, hs].bitcast(E4), lhsT_scale=h_scales[:, e, hs], rhs=b_codes[:].bitcast(E5), rhs_scale=b_scales[:], start=True, stop=True)
                 o = st.tile([P, L], F32, name="o", tag="o", bufs=4)
                 src = acc[:].rearrange("p (u q w) -> p q u w", u=2, w=2)
                 dst = o[:].rearrange("p (q u w) -> p q u w", u=2, w=2)
-                if q == 3:
-                    nc.vector.tensor_copy(out=dst, in_=src)
-                    nc.sync.dma_start(out=out_1[e, hs, :], in_=o[:])
-                else:
-                    nc.scalar.copy(out=dst, in_=src)
-                    nc.sync.dma_start(out=out_1[e, hs, :], in_=o[:])
+                nc.scalar.copy(out=dst, in_=src)
+                nc.sync.dma_start(out=out_1[e, hs, :], in_=o[:])
 
         for j in range(NPAIR):
             if j + 3 < NPAIR:

@@ -35,6 +35,9 @@ def tile_softmoedynamics_pb_v_kernel(tc, h2, logits, W3, b3, y, grad_out, out_0,
         nc.scalar.activation(out=warm[:], in_=warm[:], func=ACT.Exp)
         ident_f = keep.tile([P, P], F32, name="ident_f")
         make_identity(nc, ident_f[:])
+        swap_f = keep.tile([P, P], F32, name="swap_f")
+        for w in range(2):
+            nc.vector.tensor_copy(out=swap_f[:, w:P:2], in_=ident_f[:, 1 - w : P : 2])
 
         NCOL = 2 * NPAIR + NA
         lg = keep.tile([P, NCOL, E], BF16, name="lg")
@@ -87,7 +90,7 @@ def tile_softmoedynamics_pb_v_kernel(tc, h2, logits, W3, b3, y, grad_out, out_0,
         bd = keep.tile([P, 2 * NPAIR, P], F32, name="bd")
         CH = 4
         for c0 in range(0, 2 * NPAIR, CH):
-            eng = nc.vector if c0 < CH else nc.gpsimd
+            eng = nc.vector if c0 < 2 * CH else nc.gpsimd
             eng.tensor_tensor(
                 out=bd[:, c0 : c0 + CH, :].rearrange("p i (b e) -> p i b e", e=E),
                 in0=mask16[:].unsqueeze(1).unsqueeze(3).to_broadcast([P, CH, TOK, E]),
@@ -109,14 +112,13 @@ def tile_softmoedynamics_pb_v_kernel(tc, h2, logits, W3, b3, y, grad_out, out_0,
             pT = st.tile([P, 2, P], F32, name="pT", tag="pT", bufs=2)
             nc.scalar.copy(out=pT[:], in_=pr[:, 0:2, :])
             for a in range(2):
-                nc.tensor.transpose(pr[:, 2 + a, :], pT[:, a, :], ident_f[:])
-            p = st.tile([P, P], F32, name="p", tag="p", bufs=2)
-            nc.vector.tensor_reduce(out=p[:], in_=pr[:, 2:4, :].rearrange("p a (g w) -> p (a g) w", w=2), axis=AX.X, op=ALU.add)
+                nc.tensor.matmul(pr[:, 2 + a, :], lhsT=pT[:, a, :], rhs=ident_f[:], is_transpose=True, start=True, stop=False)
+                nc.tensor.matmul(pr[:, 2 + a, :], lhsT=pT[:, a, :], rhs=swap_f[:], is_transpose=True, start=False, stop=True)
             s = st.tile([P, 4, P, 2], F32, name="s", tag="s", bufs=2)
             nc.vector.tensor_tensor(
                 out=s[:],
                 in0=yy.rearrange("p a (g h w) -> p h (a g) w", h=4, w=2),
-                in1=p[:].unsqueeze(1).unsqueeze(3).to_broadcast([P, 4, P, 2]),
+                in1=pr[:, 2:4, :].rearrange("p a (g w) -> p (a g) w", w=2).unsqueeze(1).to_broadcast([P, 4, P, 2]),
                 op=ALU.mult,
             )
             dz = st.tile([P, 2, L], BF16, name="dz", tag="dz", bufs=3)
@@ -179,9 +181,10 @@ def tile_softmoedynamics_pb_v_kernel(tc, h2, logits, W3, b3, y, grad_out, out_0,
 
         def h_prep(e):
             h_grp = st.tile([P, H, 4], BF16, name="h_grp", tag="grp", bufs=3, align_bytes=64)
-            hr = h_raw.pop(e)
-            for c in range(4):
-                nc.gpsimd.tensor_scalar(out=h_grp[:, P * c : P * (c + 1), :], in0=hr[:, :, P * c : P * (c + 1)].rearrange("p j h -> p h j"), scalar1=1.0, scalar2=0.0, op0=ALU.mult, op1=ALU.add)
+            if e < 6:
+                nc.scalar.copy(out=h_grp[:], in_=h_raw.pop(e)[:].rearrange("p j h -> p h j"))
+            else:
+                nc.vector.tensor_copy(out=h_grp[:], in_=h_raw.pop(e)[:].rearrange("p j h -> p h j"))
             nc.vector.quantize_mx(out=h_codes[:, e, :].bitcast(E4), scales=h_scales[:, e, :], in_=h_grp[:].rearrange("p h t -> p (h t)"))
 
         ac_t = {}
@@ -209,7 +212,7 @@ def tile_softmoedynamics_pb_v_kernel(tc, h2, logits, W3, b3, y, grad_out, out_0,
         def out1(e):
             b_grp = st.tile([P, L, 4], BF16, name="b_grp", tag="grp", bufs=3, align_bytes=64)
             for u in range(2):
-                tb = ps.tile([P, 4, P], F32, name="tb", tag=("acc", "tr")[u], bufs=2)
+                tb = ps.tile([P, 4, P], F32, name="tb", tag="acc", bufs=2)
                 for s in range(4):
                     nc.tensor.transpose(tb[:, s, :], a2[:, e, u, s, :], ident_f[:])
                 nc.scalar.copy(
@@ -221,13 +224,17 @@ def tile_softmoedynamics_pb_v_kernel(tc, h2, logits, W3, b3, y, grad_out, out_0,
             nc.vector.quantize_mx(out=b_codes[:].bitcast(E5), scales=b_scales[:], in_=b_grp[:].rearrange("p l s -> p (l s)"))
             for q in range(4):
                 hs = slice(P * q, P * (q + 1))
-                acc = ps.tile([P, L], F32, name="acc1", tag=("mx", "pr")[q % 2], bufs=2)
+                acc = ps.tile([P, L], F32, name="acc1", tag="mx", bufs=2)
                 nc.tensor.matmul_mx(out=acc[:], lhsT=h_codes[:, e, hs].bitcast(E4), lhsT_scale=h_scales[:, e, hs], rhs=b_codes[:].bitcast(E5), rhs_scale=b_scales[:], start=True, stop=True)
                 o = st.tile([P, L], F32, name="o", tag="o", bufs=4)
                 src = acc[:].rearrange("p (u q w) -> p q u w", u=2, w=2)
                 dst = o[:].rearrange("p (q u w) -> p q u w", u=2, w=2)
-                nc.scalar.copy(out=dst, in_=src)
-                nc.sync.dma_start(out=out_1[e, hs, :], in_=o[:])
+                if q == 3:
+                    nc.vector.tensor_copy(out=dst, in_=src)
+                    nc.sync.dma_start(out=out_1[e, hs, :], in_=o[:])
+                else:
+                    nc.scalar.copy(out=dst, in_=src)
+                    nc.sync.dma_start(out=out_1[e, hs, :], in_=o[:])
 
         for j in range(NPAIR):
             if j + 3 < NPAIR:

from contextlib import ExitStack

import concourse.mybir as mybir
from concourse.masks import make_identity

B, NA, E, L, H, GRP = 512, 8, 8, 512, 512, 8
FLOPS = 2 * 2 * E * B * L * H + 2 * B * NA * E * L

F32 = mybir.dt.float32
BF16 = mybir.dt.bfloat16
U32 = mybir.dt.uint32
U8 = mybir.dt.uint8
E4 = mybir.dt.float8_e4m3fn_x4
E5 = mybir.dt.float8_e5m2_x4
ALU = mybir.AluOpType
AX = mybir.AxisListType
ACT = mybir.ActivationFunctionType

P = 128
TOK = 16
NPAIR = 12
BV = 2 * TOK * NPAIR
NG = L // GRP


def tile_softmoedynamics_pb_v_kernel(tc, h2, logits, W3, b3, y, grad_out, out_0, out_1):
    nc = tc.nc
    with ExitStack() as ctx:
        keep = ctx.enter_context(tc.tile_pool(name="keep", bufs=1))
        st = ctx.enter_context(tc.tile_pool(name="st", bufs=2))
        ps = ctx.enter_context(tc.psum_pool(name="ps", bufs=2))

        warm = keep.tile([P, 1], F32, name="warm")
        nc.vector.memset(warm[:], 0.0)
        nc.scalar.activation(out=warm[:], in_=warm[:], func=ACT.Exp)
        ident_f = keep.tile([P, P], F32, name="ident_f")
        make_identity(nc, ident_f[:])
        swap_f = keep.tile([P, P], F32, name="swap_f")
        for w in range(2):
            nc.vector.tensor_copy(out=swap_f[:, w:P:2], in_=ident_f[:, 1 - w : P : 2])

        NCOL = 2 * NPAIR + NA
        lg = keep.tile([P, NCOL, E], BF16, name="lg")
        nc.sync.dma_start(out=lg[:, 0 : 2 * NPAIR, :], in_=logits[0:BV].rearrange("(i b) n e -> (b n) i e", b=TOK))
        nc.sync.dma_start(out=lg[:, 2 * NPAIR :, :], in_=logits[BV:B])

        g_t, y_t, w_raw, h_raw = {}, {}, {}, {}

        def load_pair(j):
            g = st.tile([P, 2, L], BF16, name="g", tag="g", bufs=4)
            nc.sync.dma_start(out=g[:], in_=grad_out[32 * j : 32 * j + 32].rearrange("(a b) n l -> (b n) a l", b=TOK))
            yy = st.tile([P, 2, L], F32, name="yy", tag="y", bufs=4)
            nc.sync.dma_start(out=yy[:], in_=y[32 * j : 32 * j + 32].rearrange("(a b) e l -> (b e) a l", b=TOK))
            g_t[j] = g
            y_t[j] = yy

        def load_w(e):
            w = st.tile([P, 4, L], BF16, name="w_raw", tag="w_raw", bufs=2)
            nc.sync.dma_start(out=w[:], in_=W3[e].rearrange("(q p) l -> p q l", p=P))
            w_raw[e] = w

        def load_h(e):
            hh = st.tile([P, 4, H], BF16, name="h_raw", tag="h_raw", bufs=2)
            nc.sync.dma_start(out=hh[:], in_=h2[:, e, :].rearrange("(p j) h -> p j h", j=4))
            h_raw[e] = hh

        load_w(0)
        load_pair(0)
        load_w(1)
        g_v = keep.tile([P, NA, L], BF16, name="g_v")
        nc.sync.dma_start(out=g_v[:], in_=grad_out[BV:B])
        load_pair(1)
        load_pair(2)

        mx = keep.tile([P, NCOL], F32, name="mx")
        nc.vector.tensor_reduce(out=mx[:], in_=lg[:], axis=AX.X, op=ALU.max)
        sh = keep.tile([P, NCOL, E], F32, name="sh")
        nc.vector.tensor_tensor(out=sh[:], in0=lg[:], in1=mx[:].unsqueeze(2).to_broadcast([P, NCOL, E]), op=ALU.subtract)
        ex = keep.tile([P, NCOL, E], F32, name="ex")
        nc.scalar.activation(out=ex[:], in_=sh[:], func=ACT.Exp)
        sm = keep.tile([P, NCOL], F32, name="sm")
        nc.vector.tensor_reduce(out=sm[:], in_=ex[:], axis=AX.X, op=ALU.add)
        rc = keep.tile([P, NCOL], F32, name="rc")
        nc.vector.reciprocal(out=rc[:], in_=sm[:])
        cb = keep.tile([P, NCOL, E], F32, name="cb")
        nc.vector.tensor_tensor(out=cb[:], in0=ex[:], in1=rc[:].unsqueeze(2).to_broadcast([P, NCOL, E]), op=ALU.mult)

        mask16 = keep.tile([P, TOK], F32, name="mask16")
        nc.vector.tensor_reduce(out=mask16[:], in_=ident_f[:].rearrange("p (b n) -> p b n", n=NA), axis=AX.X, op=ALU.add)
        bd = keep.tile([P, 2 * NPAIR, P], F32, name="bd")
        CH = 4
        for c0 in range(0, 2 * NPAIR, CH):
            eng = nc.vector if c0 < 2 * CH else nc.gpsimd
            eng.tensor_tensor(
                out=bd[:, c0 : c0 + CH, :].rearrange("p i (b e) -> p i b e", e=E),
                in0=mask16[:].unsqueeze(1).unsqueeze(3).to_broadcast([P, CH, TOK, E]),
                in1=cb[:, c0 : c0 + CH, :].unsqueeze(2).to_broadcast([P, CH, TOK, E]),
                op=ALU.mult,
            )

        a2 = keep.tile([P, E, 2, 4, P], F32, name="a2")
        w_codes = keep.tile([P, E, H], U32, name="w_codes", align_bytes=64)
        w_scales = keep.tile([P, E, H], U8, name="w_scales", align_bytes=64)
        h_codes = keep.tile([P, E, H], U32, name="h_codes", align_bytes=64)
        h_scales = keep.tile([P, E, H], U8, name="h_scales", align_bytes=64)

        def finish_dz(t, yy):
            pr = ps.tile([P, 4, P], F32, name="pr", tag="pr", bufs=2)
            for a in range(2):
                for h in range(4):
                    nc.tensor.matmul(pr[:, a, :], lhsT=t[:, h, a, :], rhs=ident_f[:], is_transpose=True, start=(h == 0), stop=(h == 3))
            pT = st.tile([P, 2, P], F32, name="pT", tag="pT", bufs=2)
            nc.scalar.copy(out=pT[:], in_=pr[:, 0:2, :])
            for a in range(2):
                nc.tensor.matmul(pr[:, 2 + a, :], lhsT=pT[:, a, :], rhs=ident_f[:], is_transpose=True, start=True, stop=False)
                nc.tensor.matmul(pr[:, 2 + a, :], lhsT=pT[:, a, :], rhs=swap_f[:], is_transpose=True, start=False, stop=True)
            s = st.tile([P, 4, P, 2], F32, name="s", tag="s", bufs=2)
            nc.vector.tensor_tensor(
                out=s[:],
                in0=yy.rearrange("p a (g h w) -> p h (a g) w", h=4, w=2),
                in1=pr[:, 2:4, :].rearrange("p a (g w) -> p (a g) w", w=2).unsqueeze(1).to_broadcast([P, 4, P, 2]),
                op=ALU.mult,
            )
            dz = st.tile([P, 2, L], BF16, name="dz", tag="dz", bufs=3)
            nc.vector.tensor_tensor(
                out=dz[:].rearrange("p a (g h w) -> p (a g) h w", h=4, w=2),
                in0=t[:].rearrange("p h a (g w) -> p (a g) h w", w=2),
                in1=s[:].rearrange("p h x w -> p x h w"),
                op=ALU.subtract,
            )
            return dz

        def to_features(dz):
            words = dz[:].rearrange("p a l -> p (a l)").bitcast(F32)
            tr = ps.tile([P, 2, 2 * P], F32, name="tr", tag="tr", bufs=2)
            for a in range(2):
                for u in range(2):
                    nc.tensor.transpose(tr[:, u, P * a : P * (a + 1)], words[:, 256 * a + u : 256 * (a + 1) : 2], ident_f[:])
            return tr

        ag_t = {}

        def a_block(beta):
            if beta not in ag_t:
                a_new = st.tile([P, E, P, 4], BF16, name="a_grp", tag="a_grp", bufs=2, align_bytes=64)
                ag_t[beta] = a_new
            return ag_t[beta]

        def pe_pair(j):
            g, yy = g_t.pop(j), y_t.pop(j)
            t = st.tile([P, 4, 2, P], F32, name="t", tag="t", bufs=3)
            for a in range(2):
                g32 = st.tile([P, L], F32, name="g32", tag="g32", bufs=3)
                nc.scalar.copy(out=g32[:].rearrange("p (h g w) -> p h g w", h=4, w=2), in_=g[:, a, :].rearrange("p (g h w) -> p h g w", h=4, w=2))
                dy = ps.tile([P, L], F32, name="dy", tag="acc", bufs=2)
                nc.tensor.matmul(dy[:], lhsT=bd[:, 2 * j + a, :], rhs=g32[:], start=True, stop=True)
                nc.vector.tensor_tensor(
                    out=t[:, :, a, :].rearrange("p h (g w) -> p h g w", w=2),
                    in0=dy[:].rearrange("p (h g w) -> p h g w", h=4, w=2),
                    in1=yy[:, a, :].rearrange("p (g h w) -> p h g w", h=4, w=2),
                    op=ALU.mult,
                )
            dz = finish_dz(t, yy[:])
            tr = to_features(dz)
            c0 = 32 * (j % 4)
            nc.scalar.copy(out=a_block(j // 4)[:].bitcast(F32)[:, :, c0 : c0 + 32, :], in_=tr[:].rearrange("p u (c e) -> p e c u", e=E))
            for u in range(2):
                nc.scalar.copy(out=a2[:, :, u, :, 8 * j : 8 * j + 8], in_=tr[:, u, :].rearrange("p (x s e) -> p e s x", s=4, e=E))

        def w_prep(e):
            words = w_raw.pop(e)[:].rearrange("p q l -> p (q l)").bitcast(F32)
            w_grp = st.tile([P, H, 4], BF16, name="w_grp", tag="grp", bufs=3, align_bytes=64)
            for k in range(2):
                tr = ps.tile([P, 2, 2 * P], F32, name="tr", tag="tr", bufs=2)
                for a in range(2):
                    q = 2 * k + a
                    for u in range(2):
                        nc.tensor.transpose(tr[:, u, P * a : P * (a + 1)], words[:, 256 * q + u : 256 * (q + 1) : 2], ident_f[:])
                nc.scalar.copy(out=w_grp[:].bitcast(F32)[:, 256 * k : 256 * (k + 1), :], in_=tr[:].rearrange("p u c -> p c u"))
            nc.vector.quantize_mx(out=w_codes[:, e, :].bitcast(E4), scales=w_scales[:, e, :], in_=w_grp[:].rearrange("p h t -> p (h t)"))

        def h_prep(e):
            h_grp = st.tile([P, H, 4], BF16, name="h_grp", tag="grp", bufs=3, align_bytes=64)
            if e < 6:
                nc.scalar.copy(out=h_grp[:], in_=h_raw.pop(e)[:].rearrange("p j h -> p h j"))
            else:
                nc.vector.tensor_copy(out=h_grp[:], in_=h_raw.pop(e)[:].rearrange("p j h -> p h j"))
            nc.vector.quantize_mx(out=h_codes[:, e, :].bitcast(E4), scales=h_scales[:, e, :], in_=h_grp[:].rearrange("p h t -> p (h t)"))

        ac_t = {}

        def a_quant(beta, e0, ne):
            if beta not in ac_t:
                c_new = st.tile([P, E, P], U32, name="a_codes", tag="a_codes", bufs=2, align_bytes=64)
                s_new = st.tile([P, E, P], U8, name="a_scales", tag="a_scales", bufs=2, align_bytes=64)
                ac_t[beta] = (c_new, s_new)
            a_codes, a_scales = ac_t[beta]
            nc.vector.quantize_mx(
                out=a_codes[:, e0 : e0 + ne, :].rearrange("p e b -> p (e b)").bitcast(E5),
                scales=a_scales[:, e0 : e0 + ne, :].rearrange("p e b -> p (e b)"),
                in_=ag_t[beta][:, e0 : e0 + ne, :, :].rearrange("p e b t -> p (e b t)"),
            )

        def out0(beta, e):
            a_codes, a_scales = ac_t[beta]
            acc = ps.tile([P, H], F32, name="acc0", tag="mx", bufs=2)
            nc.tensor.matmul_mx(out=acc[:], lhsT=a_codes[:, e, :].bitcast(E5), lhsT_scale=a_scales[:, e, :], rhs=w_codes[:, e, :].bitcast(E4), rhs_scale=w_scales[:, e, :], start=True, stop=True)
            o = st.tile([P, H], F32, name="o", tag="o", bufs=4)
            nc.scalar.copy(out=o[:], in_=acc[:])
            nc.sync.dma_start(out=out_0[P * beta : P * (beta + 1), e, :], in_=o[:])

        def out1(e):
            b_grp = st.tile([P, L, 4], BF16, name="b_grp", tag="grp", bufs=3, align_bytes=64)
            for u in range(2):
                tb = ps.tile([P, 4, P], F32, name="tb", tag="acc", bufs=2)
                for s in range(4):
                    nc.tensor.transpose(tb[:, s, :], a2[:, e, u, s, :], ident_f[:])
                nc.scalar.copy(
                    out=b_grp[:, 256 * u : 256 * (u + 1), :].rearrange("p (q w) s -> p q w s", w=2),
                    in_=tb[:].rearrange("p s q -> p (s q)").bitcast(BF16).rearrange("p (s q w) -> p q w s", s=4, w=2),
                )
            b_codes = st.tile([P, L], U32, name="b_codes", tag="b_codes", bufs=2, align_bytes=64)
            b_scales = st.tile([P, L], U8, name="b_scales", tag="b_scales", bufs=2, align_bytes=64)
            nc.vector.quantize_mx(out=b_codes[:].bitcast(E5), scales=b_scales[:], in_=b_grp[:].rearrange("p l s -> p (l s)"))
            for q in range(4):
                hs = slice(P * q, P * (q + 1))
                acc = ps.tile([P, L], F32, name="acc1", tag="mx", bufs=2)
                nc.tensor.matmul_mx(out=acc[:], lhsT=h_codes[:, e, hs].bitcast(E4), lhsT_scale=h_scales[:, e, hs], rhs=b_codes[:].bitcast(E5), rhs_scale=b_scales[:], start=True, stop=True)
                o = st.tile([P, L], F32, name="o", tag="o", bufs=4)
                src = acc[:].rearrange("p (u q w) -> p q u w", u=2, w=2)
                dst = o[:].rearrange("p (q u w) -> p q u w", u=2, w=2)
                if q == 3:
                    nc.vector.tensor_copy(out=dst, in_=src)
                    nc.sync.dma_start(out=out_1[e, hs, :], in_=o[:])
                else:
                    nc.scalar.copy(out=dst, in_=src)
                    nc.sync.dma_start(out=out_1[e, hs, :], in_=o[:])

        for j in range(NPAIR):
            if j + 3 < NPAIR:
                load_pair(j + 3)
            pe_pair(j)
            if j < 4:
                for e in (2 * j, 2 * j + 1):
                    w_prep(e)
                    if e + 2 < E:
                        load_w(e + 2)
                    else:
                        load_h(e + 2 - E)
            else:
                h_prep(j - 4)
                if j - 4 + 2 < E:
                    load_h(j - 4 + 2)
            if j % 4 == 3:
                a_quant(j // 4, 0, E)
                for e in range(E):
                    out0(j // 4, e)

        for ep in range(E // 2):
            yv = st.tile([P, 2, L], F32, name="yv", tag="y", bufs=4)
            nc.sync.dma_start(out=yv[:], in_=y[BV:B, 2 * ep : 2 * ep + 2, :])
            dyv = st.tile([P, 2, L], F32, name="dyv", tag="dyv", bufs=3)
            for n in range(NA):
                for a in range(2):
                    c = cb[:, 2 * NPAIR + n, 2 * ep + a : 2 * ep + a + 1]
                    if n == 0:
                        nc.vector.tensor_scalar(out=dyv[:, a, :], in0=g_v[:, n, :], scalar1=c, scalar2=None, op0=ALU.mult)
                    else:
                        nc.vector.scalar_tensor_tensor(out=dyv[:, a, :], in0=g_v[:, n, :], scalar=c, in1=dyv[:, a, :], op0=ALU.mult, op1=ALU.add)
            t = st.tile([P, 4, 2, P], F32, name="t", tag="t", bufs=3)
            nc.vector.tensor_tensor(
                out=t[:].rearrange("p h a (g w) -> p h (a g) w", w=2),
                in0=dyv[:].rearrange("p a (g h w) -> p h (a g) w", h=4, w=2),
                in1=yv[:].rearrange("p a (g h w) -> p h (a g) w", h=4, w=2),
                op=ALU.mult,
            )
            dz = finish_dz(t, yv[:])
            tr = to_features(dz)
            nc.scalar.copy(out=a_block(3)[:].bitcast(F32)[:, 2 * ep : 2 * ep + 2, :, :], in_=tr[:].rearrange("p u (a b) -> p a b u", a=2))
            for u in range(2):
                nc.scalar.copy(out=a2[:, 2 * ep : 2 * ep + 2, u, :, 96:P], in_=tr[:, u, :].rearrange("p (a x s) -> p a s x", a=2, s=4))
            a_quant(3, 2 * ep, 2)
            for a in range(2):
                out0(3, 2 * ep + a)
                out1(2 * ep + a)
